import numpy as np
import ml_dtypes


def mxq(x, axis, fmt="e4m3"):
    dtype, down = {"e4m3": (ml_dtypes.float8_e4m3fn, 7), "e5m2": (ml_dtypes.float8_e5m2, 14)}[fmt]
    v = np.moveaxis(np.asarray(x, np.float32).astype(ml_dtypes.bfloat16).astype(np.float64), axis, -1)
    blocks = v.reshape(v.shape[:-1] + (-1, 32))
    amax = np.abs(blocks).max(-1, keepdims=True)
    byte = np.maximum(np.where(amax > 0, np.frexp(amax)[1] - 1 + 127, 0) - down, 1)
    scale = np.exp2(byte - 127.0)
    codes = (blocks / scale).astype(np.float32).astype(dtype).astype(np.float64)
    return np.moveaxis((codes * scale).reshape(v.shape), -1, axis)


WIDE = False


def mx_kscale(k):
    if not WIDE:
        return np.ones(k)
    levels = np.array([10, -10, 5, -5, 0])
    a = np.random.permutation(np.resize(levels, k // 512 * 4)).reshape(k // 512, 4)
    idx = np.arange(k)
    return np.exp2(a[idx // 512, idx % 128 // 32])


BF16 = ml_dtypes.bfloat16


def bf(x):
    return np.asarray(x, np.float32).astype(BF16)


def f64(x):
    return np.asarray(x).astype(np.float64)


E2M1 = np.array([0.0, 0.5, 1.0, 1.5, 2.0, 3.0, 4.0, 6.0, -0.0, -0.5, -1.0, -1.5, -2.0, -3.0, -4.0, -6.0])


def pack_weight(w, fmt):
    k, n = w.shape
    w = f64(bf(w)).reshape(k // 32, 32, n)
    amax = np.abs(w).max(1)
    if fmt == "e4m3":
        byte = np.frexp(amax)[1] - 1 + 127 - 7
    else:
        mant, ex = np.frexp(amax / 6.0)
        byte = np.where(mant > 0.5, ex, ex - 1) + 127
    byte = np.clip(np.where(amax > 0, byte, 1), 1, 254)
    scaled = (w * np.exp2(127.0 - byte)[:, None, :]).reshape(k, n).astype(np.float32)
    by_word = np.ascontiguousarray(scaled.reshape(k // 512, 128, 4, n).transpose(0, 1, 3, 2))
    if fmt == "e4m3":
        words = by_word.astype(ml_dtypes.float8_e4m3fn).view(np.uint8)
    else:
        c = by_word.astype(ml_dtypes.float4_e2m1fn).view(np.uint8) & 0xF
        words = c[..., 0::2] | (c[..., 1::2] << 4)
    return np.ascontiguousarray(words), np.ascontiguousarray(byte.astype(np.uint8).reshape(k // 512, 16, n))


def unpack_weight(words, scales, fmt):
    g, p, n, _ = words.shape
    if fmt == "e4m3":
        vals = np.ascontiguousarray(words).view(ml_dtypes.float8_e4m3fn).astype(np.float64)
    else:
        nib = np.empty((g, p, n, 4), np.uint8)
        nib[..., 0::2] = words & 0xF
        nib[..., 1::2] = words >> 4
        vals = E2M1[nib]
    vals = vals * np.repeat(np.exp2(scales.astype(np.float64) - 127.0), 8, axis=1)[..., None]
    return vals.transpose(0, 1, 3, 2).reshape(g * 512, n)


N, CI, CO, V, T = 1, 4096, 4096, 128, 1


def normalize_adjacency(adj):
    G = adj + np.eye(adj.shape[0])
    return G / G.sum(axis=1, keepdims=True)


def setup_inputs():
    s = mx_kscale(CI)
    adj = 0.1 * np.random.uniform(size=(V, V))
    i = np.arange(V - 1)
    adj[i, i + 1] += 1.0
    adj[i + 1, i] += 1.0
    x = bf(np.random.standard_normal((N, CI, V, T)) * s[None, :, None, None])
    A = bf(normalize_adjacency(adj))
    w = np.random.standard_normal((CO, CI)) * 4.0 / np.sqrt(CI) / s[None, :]
    W_words, W_scales = pack_weight(np.ascontiguousarray(w.T), "e4m3")
    b = bf(np.random.standard_normal(CO) * 0.5)
    return {"x": x,
            "A": A,
            "W_words": W_words,
            "W_scales": W_scales,
            "b": b}


def reference(x, A, W_words, W_scales, b):
    agg = (f64(x).transpose(0, 1, 3, 2) @ f64(A)).transpose(0, 1, 3, 2)
    aq = mxq(agg, 1, "e4m3")
    out = (unpack_weight(W_words, W_scales, "e4m3").T @ aq.reshape(N, CI, V * T)).reshape(N, CO, V, T)
    return out + f64(b)[None, :, None, None]

@@ -1,0 +1,149 @@
+from contextlib import ExitStack
+
+import concourse.mybir as mybir
+from concourse.masks import make_identity
+
+FLOPS = 2 * 4096 * 128 * 128 + 2 * 4096 * 4096 * 128
+
+BF16 = mybir.dt.bfloat16
+F32 = mybir.dt.float32
+I32 = mybir.dt.int32
+U32 = mybir.dt.uint32
+U8 = mybir.dt.uint8
+FP8X4 = mybir.dt.float8_e4m3fn_x4
+ADD = mybir.AluOpType.add
+IDENT = mybir.ActivationFunctionType.Identity
+
+P = 128
+G = 8
+V = 128
+CO = 4096
+CHUNKS = ((0, 2048), (2048, 1024), (3072, 1024))
+
+
+def tile_graphconv_w_kernel(tc, x, A, W_words, W_scales, b, out):
+    nc = tc.nc
+    with ExitStack() as ctx:
+        keep = ctx.enter_context(tc.tile_pool(name="keep", bufs=1))
+        psum = ctx.enter_context(tc.psum_pool(name="psum", bufs=8))
+        ctx.enter_context(tc.manual_schedule())
+
+        planes = keep.tile([P, 2, CO], U8, name="planes", align_bytes=64)
+        for a in range(2):
+            nc.vector.memset(planes[:, a, :].bitcast(I32), 0)
+        b_rows = keep.tile([P, P], BF16, name="b_rows")
+        nc.vector.memset(b_rows[:], 0.0)
+        ident = keep.tile([P, P], BF16, name="ident")
+        make_identity(nc, ident[:])
+
+        xv = x.rearrange("a c v b -> (a c) (v b)").rearrange("(g p t) v -> p g (t v)", g=G, p=P, t=4)
+        x_sb = []
+        for i in range(4):
+            xt = keep.tile([P, 2, 4 * V], BF16, name="x%d" % i)
+            nc.sync.dma_start(out=xt[:], in_=xv[:, 2 * i:2 * i + 2, :])
+            x_sb.append(xt)
+        a_sb = keep.tile([P, V], BF16, name="a_sb")
+        nc.scalar.dma_start(out=a_sb[:], in_=A)
+        nc.scalar.dma_start(out=b_rows[0:32, :], in_=b.rearrange("(j p) -> j p", p=P))
+
+        for a in range(2):
+            for q in (0, 2, 1, 3):
+                nc.sync.dma_start(
+                    out=planes[32 * q:32 * q + 16, a, :].bitcast(I32),
+                    in_=W_scales[4 * a:4 * a + 4, 4 * q:4 * q + 4, :].bitcast(I32),
+                )
+
+        w_sb = []
+        for c, (n0, nw) in enumerate(CHUNKS):
+            row = []
+            for g in range(G):
+                wt = keep.tile([P, 4 * nw], U8, name="w%d_%d" % (c, g), align_bytes=64)
+                nc.sync.dma_start(
+                    out=wt[:].bitcast(I32),
+                    in_=W_words[g].rearrange("p n t -> p (n t)")[:, 4 * n0:4 * (n0 + nw)].bitcast(I32),
+                )
+                row.append(wt)
+            w_sb.append(row)
+
+        acodes = keep.tile([P, G, V], U32, name="acodes", align_bytes=64)
+        aplane = keep.tile([P, G, V], U8, name="aplane", align_bytes=64)
+        grp = [keep.tile([P, 4, V, 4], BF16, name="grp%d" % h, align_bytes=64) for h in range(2)]
+        xT = [keep.tile([P, 8, P], BF16, name="xT%d" % i) for i in range(4)]
+        bias = keep.tile([P, 32], F32, name="bias")
+
+        def flip(i):
+            tp = psum.tile([P, 8, P], BF16, name="tp", tag="bank")
+            for u in range(8):
+                nc.tensor.transpose(tp[:, u, :], x_sb[i][:, u // 4, V * (u % 4):V * (u % 4 + 1)], ident[:])
+            if i % 2 == 0:
+                nc.vector.tensor_copy(out=xT[i][:], in_=tp[:])
+            else:
+                nc.scalar.copy(out=xT[i][:], in_=tp[:])
+
+        def aggregate(i):
+            for gl in range(2):
+                g = 2 * i + gl
+                ag = psum.tile([P, 4, V], F32, name="ag", tag="bank")
+                for t in range(4):
+                    nc.tensor.matmul(ag[:, t, :], lhsT=xT[i][:, 4 * gl + t, :], rhs=a_sb[:], start=True, stop=True)
+                dst = grp[g // 4][:, g % 4, :, :]
+                src = ag[:].rearrange("p t w -> p w t")
+                if gl == 0:
+                    nc.vector.tensor_copy(out=dst, in_=src)
+                else:
+                    nc.scalar.copy(out=dst, in_=src)
+
+        def quantise(h):
+            nc.vector.quantize_mx(
+                out=acodes[:, 4 * h:4 * h + 4, :].rearrange("p g w -> p (g w)").bitcast(FP8X4),
+                scales=aplane[:, 4 * h:4 * h + 4, :].rearrange("p g w -> p (g w)"),
+                in_=grp[h][:].rearrange("p g w t -> p (g w t)"),
+            )
+
+        flip(0)
+        flip(1)
+        aggregate(0)
+        flip(2)
+        aggregate(1)
+        flip(3)
+        aggregate(2)
+        quantise(0)
+        bt = psum.tile([P, P], BF16, name="bt", tag="bank")
+        nc.tensor.transpose(bt[:], b_rows[:], ident[:])
+        nc.vector.tensor_copy(out=bias[:], in_=bt[:, 0:32])
+        aggregate(3)
+        quantise(1)
+
+        o_sb = [keep.tile([P, 8, V], F32, name="o%d" % k) for k in range(4)]
+
+        def eight_tiles(k, tiles, col0):
+            accs = [psum.tile([P, V], F32, name="acc%d" % j, tag="bank") for j in range(8)]
+            for g in range(G):
+                for j in range(8):
+                    jj = 8 * k + j
+                    nc.tensor.matmul_mx(
+                        out=accs[j][:],
+                        lhsT=tiles[g][:, 512 * (col0 + j):512 * (col0 + j + 1)].bitcast(FP8X4),
+                        lhsT_scale=planes[4 * (g % 4):P, g // 4, P * jj:P * (jj + 1)],
+                        rhs=acodes[:, g, :].bitcast(FP8X4),
+                        rhs_scale=aplane[:, g, :],
+                        start=(g == 0),
+                        stop=(g == G - 1),
+                    )
+            for j in range(8):
+                jj = 8 * k + j
+                if j % 2 == 0:
+                    nc.scalar.activation(out=o_sb[k][:, j, :], in_=accs[j][:], func=IDENT,
+                                         bias=bias[:, jj:jj + 1], scale=1.0)
+                else:
+                    nc.vector.tensor_scalar(out=o_sb[k][:, j, :], in0=accs[j][:], scalar1=bias[:, jj:jj + 1],
+                                            scalar2=None, op0=ADD)
+
+        eight_tiles(0, w_sb[0], 0)
+        eight_tiles(1, w_sb[0], 8)
+        eight_tiles(2, w_sb[1], 0)
+        eight_tiles(3, w_sb[2], 0)
+
+        ov = out.rearrange("a o w b -> (a o) (w b)").rearrange("(j p) w -> p j w", p=P)
+        for k in range(4):
+            nc.sync.dma_start(out=ov[:, 8 * k:8 * k + 8, :], in_=o_sb[k][:])

@@ -12,13 +12,14 @@ U32 = mybir.dt.uint32
 U8 = mybir.dt.uint8
 FP8X4 = mybir.dt.float8_e4m3fn_x4
 ADD = mybir.AluOpType.add
-IDENT = mybir.ActivationFunctionType.Identity
 
 P = 128
 G = 8
 V = 128
 CO = 4096
-CHUNKS = ((0, 2048), (2048, 1024), (3072, 1024))
+PIECES = (
+    (0, 0, 4096), (1, 0, 4096), (2, 0, 4096), (3, 0, 4096), (4, 0, 4096), (5, 0, 4096),
+    (6, 0, 2048), (7, 0, 2048), (6, 2048, 2048), (7, 2048, 1024), (7, 3072, 1024))
 
 
 def tile_graphconv_w_kernel(tc, x, A, W_words, W_scales, b, out):
@@ -31,10 +32,12 @@ def tile_graphconv_w_kernel(tc, x, A, W_words, W_scales, b, out):
         planes = keep.tile([P, 2, CO], U8, name="planes", align_bytes=64)
         for a in range(2):
             nc.vector.memset(planes[:, a, :].bitcast(I32), 0)
-        b_rows = keep.tile([P, P], BF16, name="b_rows")
+        b_rows = keep.tile([P, 512], BF16, name="b_rows")
         nc.vector.memset(b_rows[:], 0.0)
         ident = keep.tile([P, P], BF16, name="ident")
         make_identity(nc, ident[:])
+        ident32 = keep.tile([P, P], F32, name="ident32")
+        make_identity(nc, ident32[:])
 
         xv = x.rearrange("a c v b -> (a c) (v b)").rearrange("(g p t) v -> p g (t v)", g=G, p=P, t=4)
         x_sb = []
@@ -44,7 +47,7 @@ def tile_graphconv_w_kernel(tc, x, A, W_words, W_scales, b, out):
             x_sb.append(xt)
         a_sb = keep.tile([P, V], BF16, name="a_sb")
         nc.scalar.dma_start(out=a_sb[:], in_=A)
-        nc.scalar.dma_start(out=b_rows[0:32, :], in_=b.rearrange("(j p) -> j p", p=P))
+        nc.scalar.dma_start(out=b_rows[0:8, :], in_=b.rearrange("(c n) -> c n", n=512))
 
         for a in range(2):
             for q in (0, 2, 1, 3):
@@ -54,22 +57,20 @@ def tile_graphconv_w_kernel(tc, x, A, W_words, W_scales, b, out):
                 )
 
         w_sb = []
-        for c, (n0, nw) in enumerate(CHUNKS):
-            row = []
-            for g in range(G):
-                wt = keep.tile([P, 4 * nw], U8, name="w%d_%d" % (c, g), align_bytes=64)
-                nc.sync.dma_start(
-                    out=wt[:].bitcast(I32),
-                    in_=W_words[g].rearrange("p n t -> p (n t)")[:, 4 * n0:4 * (n0 + nw)].bitcast(I32),
-                )
-                row.append(wt)
-            w_sb.append(row)
+        for n, (g, n0, nw) in enumerate(PIECES):
+            wt = keep.tile([P, 4 * nw], U8, name="w%d" % n, align_bytes=64)
+            nc.sync.dma_start(
+                out=wt[:].bitcast(I32),
+                in_=W_words[g].rearrange("p n t -> p (n t)")[:, 4 * n0:4 * (n0 + nw)].bitcast(I32),
+            )
+            w_sb.append(wt)
 
         acodes = keep.tile([P, G, V], U32, name="acodes", align_bytes=64)
         aplane = keep.tile([P, G, V], U8, name="aplane", align_bytes=64)
         grp = [keep.tile([P, 4, V, 4], BF16, name="grp%d" % h, align_bytes=64) for h in range(2)]
         xT = [keep.tile([P, 8, P], BF16, name="xT%d" % i) for i in range(4)]
-        bias = keep.tile([P, 32], F32, name="bias")
+        bias = keep.tile([P, 8, 4], F32, name="bias")
+        b_sorted = keep.tile([P, 4, P], BF16, name="b_sorted")
 
         def flip(i):
             tp = psum.tile([P, 8, P], BF16, name="tp", tag="bank")
@@ -108,42 +109,47 @@ def tile_graphconv_w_kernel(tc, x, A, W_words, W_scales, b, out):
         flip(3)
         aggregate(2)
         quantise(0)
-        bt = psum.tile([P, P], BF16, name="bt", tag="bank")
-        nc.tensor.transpose(bt[:], b_rows[:], ident[:])
-        nc.vector.tensor_copy(out=bias[:], in_=bt[:, 0:32])
+        nc.vector.tensor_copy(out=b_sorted[:], in_=b_rows[:].rearrange("p (i e) -> p e i", e=4))
+        bt = psum.tile([P, 4, P], BF16, name="bt", tag="bank")
+        for e in range(4):
+            nc.tensor.transpose(bt[:, e, :], b_sorted[:, e, :], ident[:])
+        nc.vector.tensor_copy(out=bias[:], in_=bt[:, :, 0:8].rearrange("p e c -> p c e"))
         aggregate(3)
         quantise(1)
 
-        o_sb = [keep.tile([P, 8, V], F32, name="o%d" % k) for k in range(4)]
+        ov = out.rearrange("a o w b -> (a o) (w b)").rearrange("(c i e) w -> c i (e w)", c=8, i=P, e=4)
+        accs = [psum.tile([P, 512], F32, name="acc%d" % c, tag="bank") for c in range(8)]
+        s_sb = [keep.tile([P, 4, P], F32, name="s%d" % c) for c in range(8)]
+        o_sb = [keep.tile([P, 4, V], F32, name="o%d" % c) for c in range(8)]
 
-        def eight_tiles(k, tiles, col0):
-            accs = [psum.tile([P, V], F32, name="acc%d" % j, tag="bank") for j in range(8)]
-            for g in range(G):
-                for j in range(8):
-                    jj = 8 * k + j
-                    nc.tensor.matmul_mx(
-                        out=accs[j][:],
-                        lhsT=tiles[g][:, 512 * (col0 + j):512 * (col0 + j + 1)].bitcast(FP8X4),
-                        lhsT_scale=planes[4 * (g % 4):P, g // 4, P * jj:P * (jj + 1)],
-                        rhs=acodes[:, g, :].bitcast(FP8X4),
-                        rhs_scale=aplane[:, g, :],
-                        start=(g == 0),
-                        stop=(g == G - 1),
-                    )
-            for j in range(8):
-                jj = 8 * k + j
-                if j % 2 == 0:
-                    nc.scalar.activation(out=o_sb[k][:, j, :], in_=accs[j][:], func=IDENT,
-                                         bias=bias[:, jj:jj + 1], scale=1.0)
-                else:
-                    nc.vector.tensor_scalar(out=o_sb[k][:, j, :], in0=accs[j][:], scalar1=bias[:, jj:jj + 1],
-                                            scalar2=None, op0=ADD)
+        def passes(n):
+            g, n0, nw = PIECES[n]
+            for col in range(nw // 512):
+                c = n0 // 512 + col
+                nc.tensor.matmul_mx(
+                    out=accs[c][:],
+                    lhsT=acodes[:, g, :].bitcast(FP8X4),
+                    lhsT_scale=aplane[:, g, :],
+                    rhs=w_sb[n][:, 2048 * col:2048 * (col + 1)].bitcast(FP8X4),
+                    rhs_scale=planes[4 * (g % 4):P, g // 4, 512 * c:512 * (c + 1)],
+                    start=(g == 0),
+                    stop=(g == G - 1),
+                )
 
-        eight_tiles(0, w_sb[0], 0)
-        eight_tiles(1, w_sb[0], 8)
-        eight_tiles(2, w_sb[1], 0)
-        eight_tiles(3, w_sb[2], 0)
+        def finish(chunks):
+            for c in chunks:
+                nc.scalar.copy(out=s_sb[c][:], in_=accs[c][:].rearrange("p (i e) -> p e i", e=4))
+            for c in chunks:
+                z = psum.tile([P, 4, V], F32, name="z", tag="bank")
+                for e in range(4):
+                    nc.tensor.transpose(z[:, e, :], s_sb[c][:, e, :], ident32[:])
+                nc.vector.tensor_tensor(out=o_sb[c][:], in0=z[:],
+                                        in1=bias[:, c, :].unsqueeze(2).to_broadcast([P, 4, V]), op=ADD)
+                nc.sync.dma_start(out=ov[c], in_=o_sb[c][:].rearrange("p e w -> p (e w)"))
 
-        ov = out.rearrange("a o w b -> (a o) (w b)").rearrange("(j p) w -> p j w", p=P)
-        for k in range(4):
-            nc.sync.dma_start(out=ov[:, 8 * k:8 * k + 8, :], in_=o_sb[k][:])
+        for n in range(8):
+            passes(n)
+        finish((0, 1, 2, 3))
+        for n in range(8, 11):
+            passes(n)
+        finish((4, 5, 6, 7))

@@ -12,14 +12,13 @@ U32 = mybir.dt.uint32
 U8 = mybir.dt.uint8
 FP8X4 = mybir.dt.float8_e4m3fn_x4
 ADD = mybir.AluOpType.add
+IDENT = mybir.ActivationFunctionType.Identity
 
 P = 128
 G = 8
 V = 128
 CO = 4096
-PIECES = (
-    (0, 0, 4096), (1, 0, 4096), (2, 0, 4096), (3, 0, 4096), (4, 0, 4096), (5, 0, 4096),
-    (6, 0, 2048), (7, 0, 2048), (6, 2048, 2048), (7, 2048, 1024), (7, 3072, 1024))
+LAST_SPLIT = 2
 
 
 def tile_graphconv_w_kernel(tc, x, A, W_words, W_scales, b, out):
@@ -32,12 +31,10 @@ def tile_graphconv_w_kernel(tc, x, A, W_words, W_scales, b, out):
         planes = keep.tile([P, 2, CO], U8, name="planes", align_bytes=64)
         for a in range(2):
             nc.vector.memset(planes[:, a, :].bitcast(I32), 0)
-        b_rows = keep.tile([P, 512], BF16, name="b_rows")
+        b_rows = keep.tile([P, P], BF16, name="b_rows")
         nc.vector.memset(b_rows[:], 0.0)
         ident = keep.tile([P, P], BF16, name="ident")
         make_identity(nc, ident[:])
-        ident32 = keep.tile([P, P], F32, name="ident32")
-        make_identity(nc, ident32[:])
 
         xv = x.rearrange("a c v b -> (a c) (v b)").rearrange("(g p t) v -> p g (t v)", g=G, p=P, t=4)
         x_sb = []
@@ -47,7 +44,7 @@ def tile_graphconv_w_kernel(tc, x, A, W_words, W_scales, b, out):
             x_sb.append(xt)
         a_sb = keep.tile([P, V], BF16, name="a_sb")
         nc.scalar.dma_start(out=a_sb[:], in_=A)
-        nc.scalar.dma_start(out=b_rows[0:8, :], in_=b.rearrange("(c n) -> c n", n=512))
+        nc.scalar.dma_start(out=b_rows[0:32, :], in_=b.rearrange("(j p) -> j p", p=P))
 
         for a in range(2):
             for q in (0, 2, 1, 3):
@@ -57,20 +54,24 @@ def tile_graphconv_w_kernel(tc, x, A, W_words, W_scales, b, out):
                 )
 
         w_sb = []
-        for n, (g, n0, nw) in enumerate(PIECES):
-            wt = keep.tile([P, 4 * nw], U8, name="w%d" % n, align_bytes=64)
-            nc.sync.dma_start(
-                out=wt[:].bitcast(I32),
-                in_=W_words[g].rearrange("p n t -> p (n t)")[:, 4 * n0:4 * (n0 + nw)].bitcast(I32),
-            )
-            w_sb.append(wt)
+        for g in range(G):
+            pieces = LAST_SPLIT if g == G - 1 else 1
+            nw = CO // pieces
+            row = []
+            for c in range(pieces):
+                wt = keep.tile([P, 4 * nw], U8, name="w%d_%d" % (g, c), align_bytes=64)
+                nc.sync.dma_start(
+                    out=wt[:].bitcast(I32),
+                    in_=W_words[g].rearrange("p n t -> p (n t)")[:, 4 * nw * c:4 * nw * (c + 1)].bitcast(I32),
+                )
+                row.append(wt)
+            w_sb.append(row)
 
         acodes = keep.tile([P, G, V], U32, name="acodes", align_bytes=64)
         aplane = keep.tile([P, G, V], U8, name="aplane", align_bytes=64)
         grp = [keep.tile([P, 4, V, 4], BF16, name="grp%d" % h, align_bytes=64) for h in range(2)]
         xT = [keep.tile([P, 8, P], BF16, name="xT%d" % i) for i in range(4)]
-        bias = keep.tile([P, 8, 4], F32, name="bias")
-        b_sorted = keep.tile([P, 4, P], BF16, name="b_sorted")
+        bias = keep.tile([P, 32], F32, name="bias")
 
         def flip(i):
             tp = psum.tile([P, 8, P], BF16, name="tp", tag="bank")
@@ -109,47 +110,38 @@ def tile_graphconv_w_kernel(tc, x, A, W_words, W_scales, b, out):
         flip(3)
         aggregate(2)
         quantise(0)
-        nc.vector.tensor_copy(out=b_sorted[:], in_=b_rows[:].rearrange("p (i e) -> p e i", e=4))
-        bt = psum.tile([P, 4, P], BF16, name="bt", tag="bank")
-        for e in range(4):
-            nc.tensor.transpose(bt[:, e, :], b_sorted[:, e, :], ident[:])
-        nc.vector.tensor_copy(out=bias[:], in_=bt[:, :, 0:8].rearrange("p e c -> p c e"))
+        bt = psum.tile([P, P], BF16, name="bt", tag="bank")
+        nc.tensor.transpose(bt[:], b_rows[:], ident[:])
+        nc.vector.tensor_copy(out=bias[:], in_=bt[:, 0:32])
         aggregate(3)
         quantise(1)
 
-        ov = out.rearrange("a o w b -> (a o) (w b)").rearrange("(c i e) w -> c i (e w)", c=8, i=P, e=4)
-        accs = [psum.tile([P, 512], F32, name="acc%d" % c, tag="bank") for c in range(8)]
-        s_sb = [keep.tile([P, 4, P], F32, name="s%d" % c) for c in range(8)]
-        o_sb = [keep.tile([P, 4, V], F32, name="o%d" % c) for c in range(8)]
-
-        def passes(n):
-            g, n0, nw = PIECES[n]
-            for col in range(nw // 512):
-                c = n0 // 512 + col
-                nc.tensor.matmul_mx(
-                    out=accs[c][:],
-                    lhsT=acodes[:, g, :].bitcast(FP8X4),
-                    lhsT_scale=aplane[:, g, :],
-                    rhs=w_sb[n][:, 2048 * col:2048 * (col + 1)].bitcast(FP8X4),
-                    rhs_scale=planes[4 * (g % 4):P, g // 4, 512 * c:512 * (c + 1)],
-                    start=(g == 0),
-                    stop=(g == G - 1),
-                )
-
-        def finish(chunks):
-            for c in chunks:
-                nc.scalar.copy(out=s_sb[c][:], in_=accs[c][:].rearrange("p (i e) -> p e i", e=4))
-            for c in chunks:
-                z = psum.tile([P, 4, V], F32, name="z", tag="bank")
-                for e in range(4):
-                    nc.tensor.transpose(z[:, e, :], s_sb[c][:, e, :], ident32[:])
-                nc.vector.tensor_tensor(out=o_sb[c][:], in0=z[:],
-                                        in1=bias[:, c, :].unsqueeze(2).to_broadcast([P, 4, V]), op=ADD)
-                nc.sync.dma_start(out=ov[c], in_=o_sb[c][:].rearrange("p e w -> p (e w)"))
-
-        for n in range(8):
-            passes(n)
-        finish((0, 1, 2, 3))
-        for n in range(8, 11):
-            passes(n)
-        finish((4, 5, 6, 7))
+        o_sb = [keep.tile([P, 4, V], F32, name="o%d" % k) for k in range(8)]
+        ov = out.rearrange("a o w b -> (a o) (w b)").rearrange("(j p) w -> p j w", p=P)
+        accs = [psum.tile([P, 4, V], F32, name="acc%d" % k, tag="bank") for k in range(8)]
+        for g in range(G):
+            per_tile = 32 // len(w_sb[g])
+            for k in range(8):
+                for s in range(4):
+                    jj = 4 * k + s
+                    wt = w_sb[g][jj // per_tile]
+                    col = jj % per_tile
+                    nc.tensor.matmul_mx(
+                        out=accs[k][:, s, :],
+                        lhsT=wt[:, 512 * col:512 * (col + 1)].bitcast(FP8X4),
+                        lhsT_scale=planes[4 * (g % 4):P, g // 4, P * jj:P * (jj + 1)],
+                        rhs=acodes[:, g, :].bitcast(FP8X4),
+                        rhs_scale=aplane[:, g, :],
+                        start=(g == 0 and s == 0),
+                        stop=(g == G - 1 and s == 3),
+                    )
+                if g == G - 1:
+                    if k % 2 == 0:
+                        nc.vector.tensor_tensor(
+                            out=o_sb[k][:], in0=accs[k][:],
+                            in1=bias[:, 4 * k:4 * k + 4].unsqueeze(2).to_broadcast([P, 4, V]), op=ADD)
+                    else:
+                        for s in range(4):
+                            nc.scalar.activation(out=o_sb[k][:, s, :], in_=accs[k][:, s, :], func=IDENT,
+                                                 bias=bias[:, 4 * k + s:4 * k + s + 1], scale=1.0)
+                    nc.sync.dma_start(out=ov[:, 4 * k:4 * k + 4, :], in_=o_sb[k][:])

@@ -12,13 +12,18 @@ U32 = mybir.dt.uint32
 U8 = mybir.dt.uint8
 FP8X4 = mybir.dt.float8_e4m3fn_x4
 ADD = mybir.AluOpType.add
-IDENT = mybir.ActivationFunctionType.Identity
 
 P = 128
 G = 8
 V = 128
 CO = 4096
-LAST_SPLIT = 2
+PIECES = (
+    (0, 0, 2048), (1, 0, 2048), (2, 0, 2048), (3, 0, 2048), (4, 0, 2048), (5, 0, 2048), (6, 0, 2048), (7, 0, 2048),
+    (0, 2048, 1024), (1, 2048, 1024), (2, 2048, 1024), (3, 2048, 1024),
+    (4, 2048, 1024), (5, 2048, 1024), (6, 2048, 1024), (7, 2048, 1024),
+    (0, 3072, 1024), (1, 3072, 1024), (2, 3072, 1024), (3, 3072, 1024),
+    (4, 3072, 1024), (5, 3072, 1024), (6, 3072, 1024), (7, 3072, 512), (7, 3584, 512))
+IDENT = mybir.ActivationFunctionType.Identity
 
 
 def tile_graphconv_w_kernel(tc, x, A, W_words, W_scales, b, out):
@@ -31,10 +36,12 @@ def tile_graphconv_w_kernel(tc, x, A, W_words, W_scales, b, out):
         planes = keep.tile([P, 2, CO], U8, name="planes", align_bytes=64)
         for a in range(2):
             nc.vector.memset(planes[:, a, :].bitcast(I32), 0)
-        b_rows = keep.tile([P, P], BF16, name="b_rows")
+        b_rows = keep.tile([P, 512], BF16, name="b_rows")
         nc.vector.memset(b_rows[:], 0.0)
         ident = keep.tile([P, P], BF16, name="ident")
         make_identity(nc, ident[:])
+        ident32 = keep.tile([P, P], F32, name="ident32")
+        make_identity(nc, ident32[:])
 
         xv = x.rearrange("a c v b -> (a c) (v b)").rearrange("(g p t) v -> p g (t v)", g=G, p=P, t=4)
         x_sb = []
@@ -44,7 +51,7 @@ def tile_graphconv_w_kernel(tc, x, A, W_words, W_scales, b, out):
             x_sb.append(xt)
         a_sb = keep.tile([P, V], BF16, name="a_sb")
         nc.scalar.dma_start(out=a_sb[:], in_=A)
-        nc.scalar.dma_start(out=b_rows[0:32, :], in_=b.rearrange("(j p) -> j p", p=P))
+        nc.scalar.dma_start(out=b_rows[0:8, :], in_=b.rearrange("(c n) -> c n", n=512))
 
         for a in range(2):
             for q in (0, 2, 1, 3):
@@ -54,24 +61,21 @@ def tile_graphconv_w_kernel(tc, x, A, W_words, W_scales, b, out):
                 )
 
         w_sb = []
-        for g in range(G):
-            pieces = LAST_SPLIT if g == G - 1 else 1
-            nw = CO // pieces
-            row = []
-            for c in range(pieces):
-                wt = keep.tile([P, 4 * nw], U8, name="w%d_%d" % (g, c), align_bytes=64)
-                nc.sync.dma_start(
-                    out=wt[:].bitcast(I32),
-                    in_=W_words[g].rearrange("p n t -> p (n t)")[:, 4 * nw * c:4 * nw * (c + 1)].bitcast(I32),
-                )
-                row.append(wt)
-            w_sb.append(row)
+        for n, (g, n0, nw) in enumerate(PIECES):
+            wt = keep.tile([P, 4 * nw], U8, name="w%d" % n, align_bytes=64)
+            nc.sync.dma_start(
+                out=wt[:].bitcast(I32),
+                in_=W_words[g].rearrange("p n t -> p (n t)")[:, 4 * n0:4 * (n0 + nw)].bitcast(I32),
+            )
+            w_sb.append(wt)
 
         acodes = keep.tile([P, G, V], U32, name="acodes", align_bytes=64)
         aplane = keep.tile([P, G, V], U8, name="aplane", align_bytes=64)
         grp = [keep.tile([P, 4, V, 4], BF16, name="grp%d" % h, align_bytes=64) for h in range(2)]
         xT = [keep.tile([P, 8, P], BF16, name="xT%d" % i) for i in range(4)]
-        bias = keep.tile([P, 32], F32, name="bias")
+        bias = keep.tile([P, 8, 4], F32, name="bias")
+        bias1 = keep.tile([P, 8, 4], F32, name="bias1")
+        b_sorted = keep.tile([P, 4, P], BF16, name="b_sorted")
 
         def flip(i):
             tp = psum.tile([P, 8, P], BF16, name="tp", tag="bank")
@@ -110,38 +114,91 @@ def tile_graphconv_w_kernel(tc, x, A, W_words, W_scales, b, out):
         flip(3)
         aggregate(2)
         quantise(0)
-        bt = psum.tile([P, P], BF16, name="bt", tag="bank")
-        nc.tensor.transpose(bt[:], b_rows[:], ident[:])
-        nc.vector.tensor_copy(out=bias[:], in_=bt[:, 0:32])
+        nc.vector.tensor_copy(out=b_sorted[:], in_=b_rows[:].rearrange("p (i e) -> p e i", e=4))
+        bt = psum.tile([P, 4, P], BF16, name="bt", tag="bank")
+        for e in range(4):
+            nc.tensor.transpose(bt[:, e, :], b_sorted[:, e, :], ident[:])
+        nc.vector.tensor_copy(out=bias[:], in_=bt[:, :, 0:8].rearrange("p e c -> p c e"))
+        bt1 = psum.tile([P, 4, P], BF16, name="bt1", tag="bank")
+        for s in range(4):
+            nc.tensor.transpose(bt1[:, s, :], b_rows[:, P * s:P * (s + 1)], ident[:])
+        nc.vector.tensor_copy(out=bias1[:], in_=bt1[:, :, 0:8].rearrange("p s c -> p c s"))
         aggregate(3)
         quantise(1)
 
-        o_sb = [keep.tile([P, 4, V], F32, name="o%d" % k) for k in range(8)]
-        ov = out.rearrange("a o w b -> (a o) (w b)").rearrange("(j p) w -> p j w", p=P)
-        accs = [psum.tile([P, 4, V], F32, name="acc%d" % k, tag="bank") for k in range(8)]
-        for g in range(G):
-            per_tile = 32 // len(w_sb[g])
-            for k in range(8):
-                for s in range(4):
-                    jj = 4 * k + s
-                    wt = w_sb[g][jj // per_tile]
-                    col = jj % per_tile
-                    nc.tensor.matmul_mx(
-                        out=accs[k][:, s, :],
-                        lhsT=wt[:, 512 * col:512 * (col + 1)].bitcast(FP8X4),
-                        lhsT_scale=planes[4 * (g % 4):P, g // 4, P * jj:P * (jj + 1)],
-                        rhs=acodes[:, g, :].bitcast(FP8X4),
-                        rhs_scale=aplane[:, g, :],
-                        start=(g == 0 and s == 0),
-                        stop=(g == G - 1 and s == 3),
-                    )
-                if g == G - 1:
-                    if k % 2 == 0:
-                        nc.vector.tensor_tensor(
-                            out=o_sb[k][:], in0=accs[k][:],
-                            in1=bias[:, 4 * k:4 * k + 4].unsqueeze(2).to_broadcast([P, 4, V]), op=ADD)
-                    else:
-                        for s in range(4):
-                            nc.scalar.activation(out=o_sb[k][:, s, :], in_=accs[k][:, s, :], func=IDENT,
-                                                 bias=bias[:, 4 * k + s:4 * k + s + 1], scale=1.0)
-                    nc.sync.dma_start(out=ov[:, 4 * k:4 * k + 4, :], in_=o_sb[k][:])
+        o2 = out.rearrange("a o w b -> (a o) (w b)")
+        ov = o2.rearrange("(c i e) w -> c i (e w)", c=8, i=P, e=4)
+        ow = o2.rearrange("(c s p) w -> c p s w", c=8, s=4, p=P)
+        s_sb = [keep.tile([P, 4, P], F32, name="s%d" % c) for c in range(6)]
+        o_sb = [keep.tile([P, 4, V], F32, name="o%d" % c) for c in range(8)]
+        accs = {}
+
+        def passes(n):
+            g, n0, nw = PIECES[n]
+            for col in range(nw // 512):
+                c = n0 // 512 + col
+                if g == 0:
+                    accs[c] = psum.tile([P, 512], F32, name="acc%d" % c, tag="bank")
+                nc.tensor.matmul_mx(
+                    out=accs[c][:],
+                    lhsT=acodes[:, g, :].bitcast(FP8X4),
+                    lhsT_scale=aplane[:, g, :],
+                    rhs=w_sb[n][:, 2048 * col:2048 * (col + 1)].bitcast(FP8X4),
+                    rhs_scale=planes[4 * (g % 4):P, g // 4, 512 * c:512 * (c + 1)],
+                    start=(g == 0),
+                    stop=(g == G - 1),
+                )
+
+        def finish(chunks):
+            for c in chunks:
+                nc.scalar.copy(out=s_sb[c][:], in_=accs[c][:].rearrange("p (i e) -> p e i", e=4))
+            for c in chunks:
+                z = psum.tile([P, 4, V], F32, name="z", tag="bank")
+                for e in range(4):
+                    nc.tensor.transpose(z[:, e, :], s_sb[c][:, e, :], ident32[:])
+                nc.vector.tensor_tensor(out=o_sb[c][:], in0=z[:],
+                                        in1=bias[:, c, :].unsqueeze(2).to_broadcast([P, 4, V]), op=ADD)
+
+        direct = {}
+
+        def passes_direct(n):
+            g, n0, nw = PIECES[n]
+            for col in range(nw // P):
+                jj = n0 // P + col
+                if g == 0 and jj % 2 == 0:
+                    direct[jj // 2] = psum.tile([P, 2, V], F32, name="d%d" % (jj // 2), tag="bank")
+                nc.tensor.matmul_mx(
+                    out=direct[jj // 2][:, jj % 2, :],
+                    lhsT=w_sb[n][:, 512 * col:512 * (col + 1)].bitcast(FP8X4),
+                    lhsT_scale=planes[4 * (g % 4):P, g // 4, P * jj:P * (jj + 1)],
+                    rhs=acodes[:, g, :].bitcast(FP8X4),
+                    rhs_scale=aplane[:, g, :],
+                    start=(g == 0 and jj % 2 == 0),
+                    stop=(g == G - 1 and jj % 2 == 1),
+                )
+
+        def finish_direct(c):
+            lo = direct[2 * c]
+            hi = direct[2 * c + 1]
+            nc.vector.tensor_tensor(out=o_sb[c][:, 0:2, :], in0=lo[:],
+                                    in1=bias1[:, c, 0:2].unsqueeze(2).to_broadcast([P, 2, V]), op=ADD)
+            for s in range(2, 4):
+                nc.scalar.activation(out=o_sb[c][:, s, :], in_=hi[:, s - 2, :], func=IDENT,
+                                     bias=bias1[:, c, s:s + 1], scale=1.0)
+
+        for n in range(8):
+            passes(n)
+        finish((0, 1, 2, 3))
+        for n in range(8, 16):
+            passes(n)
+        finish((4, 5))
+        for n in range(16, 24):
+            passes_direct(n)
+        finish_direct(6)
+        passes_direct(24)
+        finish_direct(7)
+
+        for c in range(6):
+            nc.sync.dma_start(out=ov[c], in_=o_sb[c][:].rearrange("p e w -> p (e w)"))
+        for c in range(6, 8):
+            nc.sync.dma_start(out=ow[c], in_=o_sb[c][:])

@@ -36,22 +36,19 @@ def tile_graphconv_w_kernel(tc, x, A, W_words, W_scales, b, out):
         planes = keep.tile([P, 2, CO], U8, name="planes", align_bytes=64)
         for a in range(2):
             nc.vector.memset(planes[:, a, :].bitcast(I32), 0)
-        b_rows = keep.tile([P, 512], BF16, name="b_rows")
+        b_rows = keep.tile([P, 1024], BF16, name="b_rows")
         nc.vector.memset(b_rows[:], 0.0)
         ident = keep.tile([P, P], BF16, name="ident")
         make_identity(nc, ident[:])
         ident32 = keep.tile([P, P], F32, name="ident32")
         make_identity(nc, ident32[:])
 
-        xv = x.rearrange("a c v b -> (a c) (v b)").rearrange("(g p t) v -> p g (t v)", g=G, p=P, t=4)
-        x_sb = []
-        for i in range(4):
-            xt = keep.tile([P, 2, 4 * V], BF16, name="x%d" % i)
-            nc.sync.dma_start(out=xt[:], in_=xv[:, 2 * i:2 * i + 2, :])
-            x_sb.append(xt)
+        x_sb = keep.tile([P, 32, V], BF16, name="x_sb")
+        nc.sync.dma_start(out=x_sb[:].rearrange("r c v -> r (c v)"),
+                          in_=x.rearrange("a c v b -> (a c) (v b)").rearrange("(r c) v -> r (c v)", r=P))
         a_sb = keep.tile([P, V], BF16, name="a_sb")
         nc.scalar.dma_start(out=a_sb[:], in_=A)
-        nc.scalar.dma_start(out=b_rows[0:8, :], in_=b.rearrange("(c n) -> c n", n=512))
+        nc.scalar.dma_start(out=b_rows[0:4, :], in_=b.rearrange("(c n) -> c n", n=1024))
 
         for a in range(2):
             for q in (0, 2, 1, 3):
@@ -72,26 +69,28 @@ def tile_graphconv_w_kernel(tc, x, A, W_words, W_scales, b, out):
         acodes = keep.tile([P, G, V], U32, name="acodes", align_bytes=64)
         aplane = keep.tile([P, G, V], U8, name="aplane", align_bytes=64)
         grp = [keep.tile([P, 4, V, 4], BF16, name="grp%d" % h, align_bytes=64) for h in range(2)]
-        xT = [keep.tile([P, 8, P], BF16, name="xT%d" % i) for i in range(4)]
-        bias = keep.tile([P, 8, 4], F32, name="bias")
-        bias1 = keep.tile([P, 8, 4], F32, name="bias1")
-        b_sorted = keep.tile([P, 4, P], BF16, name="b_sorted")
+        xT = [keep.tile([P, G, P], BF16, name="xT%d" % t) for t in range(4)]
+        bias = keep.tile([P, 3, 8], F32, name="bias")
+        bias1 = keep.tile([P, 2, 4], F32, name="bias1")
+        b_sorted = keep.tile([P, 8, P], BF16, name="b_sorted")
 
-        def flip(i):
+        def flip(t):
             tp = psum.tile([P, 8, P], BF16, name="tp", tag="bank")
-            for u in range(8):
-                nc.tensor.transpose(tp[:, u, :], x_sb[i][:, u // 4, V * (u % 4):V * (u % 4 + 1)], ident[:])
-            if i % 2 == 0:
-                nc.vector.tensor_copy(out=xT[i][:], in_=tp[:])
+            for s in range(8):
+                nc.tensor.transpose(tp[:, s, :], x_sb[:, 4 * s + t, :], ident[:])
+            dst = xT[t][:].rearrange("v g p -> v (g p)").rearrange("v (r s) -> v r s", s=8)
+            src = tp[:].rearrange("v s r -> v r s")
+            if t % 2 == 0:
+                nc.vector.tensor_copy(out=dst, in_=src)
             else:
-                nc.scalar.copy(out=xT[i][:], in_=tp[:])
+                nc.scalar.copy(out=dst, in_=src)
 
         def aggregate(i):
             for gl in range(2):
                 g = 2 * i + gl
                 ag = psum.tile([P, 4, V], F32, name="ag", tag="bank")
                 for t in range(4):
-                    nc.tensor.matmul(ag[:, t, :], lhsT=xT[i][:, 4 * gl + t, :], rhs=a_sb[:], start=True, stop=True)
+                    nc.tensor.matmul(ag[:, t, :], lhsT=xT[t][:, g, :], rhs=a_sb[:], start=True, stop=True)
                 dst = grp[g // 4][:, g % 4, :, :]
                 src = ag[:].rearrange("p t w -> p w t")
                 if gl == 0:
@@ -106,31 +105,30 @@ def tile_graphconv_w_kernel(tc, x, A, W_words, W_scales, b, out):
                 in_=grp[h][:].rearrange("p g w t -> p (g w t)"),
             )
 
-        flip(0)
-        flip(1)
+        for t in range(4):
+            flip(t)
         aggregate(0)
-        flip(2)
         aggregate(1)
-        flip(3)
         aggregate(2)
         quantise(0)
-        nc.vector.tensor_copy(out=b_sorted[:], in_=b_rows[:].rearrange("p (i e) -> p e i", e=4))
-        bt = psum.tile([P, 4, P], BF16, name="bt", tag="bank")
-        for e in range(4):
+        nc.vector.tensor_copy(out=b_sorted[:], in_=b_rows[:].rearrange("p (i e) -> p e i", e=8))
+        bt = psum.tile([P, 8, P], BF16, name="bt", tag="bank")
+        for e in range(8):
             nc.tensor.transpose(bt[:, e, :], b_sorted[:, e, :], ident[:])
-        nc.vector.tensor_copy(out=bias[:], in_=bt[:, :, 0:8].rearrange("p e c -> p c e"))
-        bt1 = psum.tile([P, 4, P], BF16, name="bt1", tag="bank")
-        for s in range(4):
+        nc.vector.tensor_copy(out=bias[:], in_=bt[:, :, 0:3].rearrange("p e c -> p c e"))
+        bt1 = psum.tile([P, 8, P], BF16, name="bt1", tag="bank")
+        for s in range(8):
             nc.tensor.transpose(bt1[:, s, :], b_rows[:, P * s:P * (s + 1)], ident[:])
-        nc.vector.tensor_copy(out=bias1[:], in_=bt1[:, :, 0:8].rearrange("p s c -> p c s"))
+        nc.vector.tensor_copy(out=bias1[:].rearrange("p c s -> p (c s)").unsqueeze(2), in_=bt1[:, :, 3:4])
         aggregate(3)
         quantise(1)
 
         o2 = out.rearrange("a o w b -> (a o) (w b)")
-        ov = o2.rearrange("(c i e) w -> c i (e w)", c=8, i=P, e=4)
+        ov = o2.rearrange("(c i e) w -> c i (e w)", c=4, i=P, e=8)
         ow = o2.rearrange("(c s p) w -> c p s w", c=8, s=4, p=P)
-        s_sb = [keep.tile([P, 4, P], F32, name="s%d" % c) for c in range(6)]
-        o_sb = [keep.tile([P, 4, V], F32, name="o%d" % c) for c in range(8)]
+        s_sb = [keep.tile([P, 8, P], F32, name="s%d" % c) for c in range(3)]
+        o_pair = [keep.tile([P, 8, V], F32, name="op%d" % c) for c in range(3)]
+        o_sb = [keep.tile([P, 4, V], F32, name="o%d" % c) for c in range(2)]
         accs = {}
 
         def passes(n):
@@ -149,15 +147,18 @@ def tile_graphconv_w_kernel(tc, x, A, W_words, W_scales, b, out):
                     stop=(g == G - 1),
                 )
 
-        def finish(chunks):
-            for c in chunks:
-                nc.scalar.copy(out=s_sb[c][:], in_=accs[c][:].rearrange("p (i e) -> p e i", e=4))
-            for c in chunks:
-                z = psum.tile([P, 4, V], F32, name="z", tag="bank")
-                for e in range(4):
-                    nc.tensor.transpose(z[:, e, :], s_sb[c][:, e, :], ident32[:])
-                nc.vector.tensor_tensor(out=o_sb[c][:], in0=z[:],
-                                        in1=bias[:, c, :].unsqueeze(2).to_broadcast([P, 4, V]), op=ADD)
+        def finish(pairs):
+            for c in pairs:
+                for h in range(2):
+                    nc.scalar.copy(out=s_sb[c][:, :, 64 * h:64 * (h + 1)],
+                                   in_=accs[2 * c + h][:].rearrange("p (i e) -> p e i", e=8))
+            for c in pairs:
+                for h in range(2):
+                    z = psum.tile([P, 4, V], F32, name="z", tag="bank")
+                    for e in range(4):
+                        nc.tensor.transpose(z[:, e, :], s_sb[c][:, 4 * h + e, :], ident32[:])
+                    nc.vector.tensor_tensor(out=o_pair[c][:, 4 * h:4 * h + 4, :], in0=z[:],
+                                            in1=bias[:, c, 4 * h:4 * h + 4].unsqueeze(2).to_broadcast([P, 4, V]), op=ADD)
 
         direct = {}
 
@@ -180,25 +181,25 @@ def tile_graphconv_w_kernel(tc, x, A, W_words, W_scales, b, out):
         def finish_direct(c):
             lo = direct[2 * c]
             hi = direct[2 * c + 1]
-            nc.vector.tensor_tensor(out=o_sb[c][:, 0:2, :], in0=lo[:],
-                                    in1=bias1[:, c, 0:2].unsqueeze(2).to_broadcast([P, 2, V]), op=ADD)
+            nc.vector.tensor_tensor(out=o_sb[c - 6][:, 0:2, :], in0=lo[:],
+                                    in1=bias1[:, c - 6, 0:2].unsqueeze(2).to_broadcast([P, 2, V]), op=ADD)
             for s in range(2, 4):
-                nc.scalar.activation(out=o_sb[c][:, s, :], in_=hi[:, s - 2, :], func=IDENT,
-                                     bias=bias1[:, c, s:s + 1], scale=1.0)
+                nc.scalar.activation(out=o_sb[c - 6][:, s, :], in_=hi[:, s - 2, :], func=IDENT,
+                                     bias=bias1[:, c - 6, s:s + 1], scale=1.0)
 
         for n in range(8):
             passes(n)
-        finish((0, 1, 2, 3))
+        finish((0, 1))
         for n in range(8, 16):
             passes(n)
-        finish((4, 5))
+        finish((2,))
         for n in range(16, 24):
             passes_direct(n)
         finish_direct(6)
         passes_direct(24)
         finish_direct(7)
 
-        for c in range(6):
-            nc.sync.dma_start(out=ov[c], in_=o_sb[c][:].rearrange("p e w -> p (e w)"))
+        for c in range(3):
+            nc.sync.dma_start(out=ov[c], in_=o_pair[c][:].rearrange("p e w -> p (e w)"))
         for c in range(6, 8):
-            nc.sync.dma_start(out=ow[c], in_=o_sb[c][:])
+            nc.sync.dma_start(out=ow[c], in_=o_sb[c - 6][:])

@@ -18,11 +18,10 @@ G = 8
 V = 128
 CO = 4096
 PIECES = (
-    (0, 0, 2048), (1, 0, 2048), (2, 0, 2048), (3, 0, 2048), (4, 0, 2048), (5, 0, 2048), (6, 0, 2048), (7, 0, 2048),
-    (0, 2048, 1024), (1, 2048, 1024), (2, 2048, 1024), (3, 2048, 1024),
-    (4, 2048, 1024), (5, 2048, 1024), (6, 2048, 1024), (7, 2048, 1024),
-    (0, 3072, 1024), (1, 3072, 1024), (2, 3072, 1024), (3, 3072, 1024),
-    (4, 3072, 1024), (5, 3072, 1024), (6, 3072, 1024), (7, 3072, 512), (7, 3584, 512))
+    (0, 2, 0, 2048), (2, 2, 0, 2048), (4, 2, 0, 2048), (6, 2, 0, 2048),
+    (0, 2, 2048, 1024), (2, 2, 2048, 1024), (4, 2, 2048, 1024), (6, 2, 2048, 1024),
+    (0, 2, 3072, 1024), (2, 2, 3072, 1024), (4, 2, 3072, 1024),
+    (6, 1, 3072, 1024), (7, 1, 3072, 512), (7, 1, 3584, 512))
 IDENT = mybir.ActivationFunctionType.Identity
 
 
@@ -58,11 +57,11 @@ def tile_graphconv_w_kernel(tc, x, A, W_words, W_scales, b, out):
                 )
 
         w_sb = []
-        for n, (g, n0, nw) in enumerate(PIECES):
-            wt = keep.tile([P, 4 * nw], U8, name="w%d" % n, align_bytes=64)
+        for n, (g, ng, n0, nw) in enumerate(PIECES):
+            wt = keep.tile([P, ng, 4 * nw], U8, name="w%d" % n, align_bytes=64)
             nc.sync.dma_start(
                 out=wt[:].bitcast(I32),
-                in_=W_words[g].rearrange("p n t -> p (n t)")[:, 4 * n0:4 * (n0 + nw)].bitcast(I32),
+                in_=W_words[g:g + ng].rearrange("g p n t -> p g (n t)")[:, :, 4 * n0:4 * (n0 + nw)].bitcast(I32),
             )
             w_sb.append(wt)
 
@@ -132,8 +131,8 @@ def tile_graphconv_w_kernel(tc, x, A, W_words, W_scales, b, out):
         accs = {}
 
         def passes(n):
-            g, n0, nw = PIECES[n]
-            for col in range(nw // 512):
+            g0, ng, n0, nw = PIECES[n]
+            for g, col in ((g, col) for g in range(g0, g0 + ng) for col in range(nw // 512)):
                 c = n0 // 512 + col
                 if g == 0:
                     accs[c] = psum.tile([P, 512], F32, name="acc%d" % c, tag="bank")
@@ -141,7 +140,7 @@ def tile_graphconv_w_kernel(tc, x, A, W_words, W_scales, b, out):
                     out=accs[c][:],
                     lhsT=acodes[:, g, :].bitcast(FP8X4),
                     lhsT_scale=aplane[:, g, :],
-                    rhs=w_sb[n][:, 2048 * col:2048 * (col + 1)].bitcast(FP8X4),
+                    rhs=w_sb[n][:, g - g0, 2048 * col:2048 * (col + 1)].bitcast(FP8X4),
                     rhs_scale=planes[4 * (g % 4):P, g // 4, 512 * c:512 * (c + 1)],
                     start=(g == 0),
                     stop=(g == G - 1),
@@ -163,14 +162,14 @@ def tile_graphconv_w_kernel(tc, x, A, W_words, W_scales, b, out):
         direct = {}
 
         def passes_direct(n):
-            g, n0, nw = PIECES[n]
-            for col in range(nw // P):
+            g0, ng, n0, nw = PIECES[n]
+            for g, col in ((g, col) for g in range(g0, g0 + ng) for col in range(nw // P)):
                 jj = n0 // P + col
                 if g == 0 and jj % 2 == 0:
                     direct[jj // 2] = psum.tile([P, 2, V], F32, name="d%d" % (jj // 2), tag="bank")
                 nc.tensor.matmul_mx(
                     out=direct[jj // 2][:, jj % 2, :],
-                    lhsT=w_sb[n][:, 512 * col:512 * (col + 1)].bitcast(FP8X4),
+                    lhsT=w_sb[n][:, g - g0, 512 * col:512 * (col + 1)].bitcast(FP8X4),
                     lhsT_scale=planes[4 * (g % 4):P, g // 4, P * jj:P * (jj + 1)],
                     rhs=acodes[:, g, :].bitcast(FP8X4),
                     rhs_scale=aplane[:, g, :],
@@ -187,16 +186,16 @@ def tile_graphconv_w_kernel(tc, x, A, W_words, W_scales, b, out):
                 nc.scalar.activation(out=o_sb[c - 6][:, s, :], in_=hi[:, s - 2, :], func=IDENT,
                                      bias=bias1[:, c - 6, s:s + 1], scale=1.0)
 
-        for n in range(8):
+        for n in range(4):
             passes(n)
         finish((0, 1))
-        for n in range(8, 16):
+        for n in range(4, 8):
             passes(n)
         finish((2,))
-        for n in range(16, 24):
+        for n in range(8, 13):
             passes_direct(n)
         finish_direct(6)
-        passes_direct(24)
+        passes_direct(13)
         finish_direct(7)
 
         for c in range(3):

from contextlib import ExitStack

import concourse.mybir as mybir
from concourse.masks import make_identity

FLOPS = 2 * 4096 * 128 * 128 + 2 * 4096 * 4096 * 128

BF16 = mybir.dt.bfloat16
F32 = mybir.dt.float32
I32 = mybir.dt.int32
U32 = mybir.dt.uint32
U8 = mybir.dt.uint8
FP8X4 = mybir.dt.float8_e4m3fn_x4
ADD = mybir.AluOpType.add

P = 128
G = 8
V = 128
CO = 4096
PIECES = (
    (0, 2, 0, 2048), (2, 2, 0, 2048), (4, 2, 0, 2048), (6, 2, 0, 2048),
    (0, 2, 2048, 1024), (2, 2, 2048, 1024), (4, 2, 2048, 1024), (6, 2, 2048, 1024),
    (0, 2, 3072, 1024), (2, 2, 3072, 1024), (4, 2, 3072, 1024),
    (6, 1, 3072, 1024), (7, 1, 3072, 512), (7, 1, 3584, 512))
IDENT = mybir.ActivationFunctionType.Identity


def tile_graphconv_w_kernel(tc, x, A, W_words, W_scales, b, out):
    nc = tc.nc
    with ExitStack() as ctx:
        keep = ctx.enter_context(tc.tile_pool(name="keep", bufs=1))
        psum = ctx.enter_context(tc.psum_pool(name="psum", bufs=8))
        ctx.enter_context(tc.manual_schedule())

        planes = keep.tile([P, 2, CO], U8, name="planes", align_bytes=64)
        for a in range(2):
            nc.vector.memset(planes[:, a, :].bitcast(I32), 0)
        b_rows = keep.tile([P, 1024], BF16, name="b_rows")
        nc.vector.memset(b_rows[:], 0.0)
        ident = keep.tile([P, P], BF16, name="ident")
        make_identity(nc, ident[:])
        ident32 = keep.tile([P, P], F32, name="ident32")
        make_identity(nc, ident32[:])

        x_sb = keep.tile([P, 32, V], BF16, name="x_sb")
        nc.sync.dma_start(out=x_sb[:].rearrange("r c v -> r (c v)"),
                          in_=x.rearrange("a c v b -> (a c) (v b)").rearrange("(r c) v -> r (c v)", r=P))
        a_sb = keep.tile([P, V], BF16, name="a_sb")
        nc.scalar.dma_start(out=a_sb[:], in_=A)
        nc.scalar.dma_start(out=b_rows[0:4, :], in_=b.rearrange("(c n) -> c n", n=1024))

        for a in range(2):
            for q in (0, 2, 1, 3):
                nc.sync.dma_start(
                    out=planes[32 * q:32 * q + 16, a, :].bitcast(I32),
                    in_=W_scales[4 * a:4 * a + 4, 4 * q:4 * q + 4, :].bitcast(I32),
                )

        w_sb = []
        for n, (g, ng, n0, nw) in enumerate(PIECES):
            wt = keep.tile([P, ng, 4 * nw], U8, name="w%d" % n, align_bytes=64)
            nc.sync.dma_start(
                out=wt[:].bitcast(I32),
                in_=W_words[g:g + ng].rearrange("g p n t -> p g (n t)")[:, :, 4 * n0:4 * (n0 + nw)].bitcast(I32),
            )
            w_sb.append(wt)

        acodes = keep.tile([P, G, V], U32, name="acodes", align_bytes=64)
        aplane = keep.tile([P, G, V], U8, name="aplane", align_bytes=64)
        grp = [keep.tile([P, 4, V, 4], BF16, name="grp%d" % h, align_bytes=64) for h in range(2)]
        xT = [keep.tile([P, G, P], BF16, name="xT%d" % t) for t in range(4)]
        bias = keep.tile([P, 3, 8], F32, name="bias")
        bias1 = keep.tile([P, 2, 4], F32, name="bias1")
        b_sorted = keep.tile([P, 8, P], BF16, name="b_sorted")

        def flip(t):
            tp = psum.tile([P, 8, P], BF16, name="tp", tag="bank")
            for s in range(8):
                nc.tensor.transpose(tp[:, s, :], x_sb[:, 4 * s + t, :], ident[:])
            dst = xT[t][:].rearrange("v g p -> v (g p)").rearrange("v (r s) -> v r s", s=8)
            src = tp[:].rearrange("v s r -> v r s")
            if t % 2 == 0:
                nc.vector.tensor_copy(out=dst, in_=src)
            else:
                nc.scalar.copy(out=dst, in_=src)

        def aggregate(i):
            for gl in range(2):
                g = 2 * i + gl
                ag = psum.tile([P, 4, V], F32, name="ag", tag="bank")
                for t in range(4):
                    nc.tensor.matmul(ag[:, t, :], lhsT=xT[t][:, g, :], rhs=a_sb[:], start=True, stop=True)
                dst = grp[g // 4][:, g % 4, :, :]
                src = ag[:].rearrange("p t w -> p w t")
                if gl == 0:
                    nc.vector.tensor_copy(out=dst, in_=src)
                else:
                    nc.scalar.copy(out=dst, in_=src)

        def quantise(h):
            nc.vector.quantize_mx(
                out=acodes[:, 4 * h:4 * h + 4, :].rearrange("p g w -> p (g w)").bitcast(FP8X4),
                scales=aplane[:, 4 * h:4 * h + 4, :].rearrange("p g w -> p (g w)"),
                in_=grp[h][:].rearrange("p g w t -> p (g w t)"),
            )

        for t in range(4):
            flip(t)
        aggregate(0)
        aggregate(1)
        aggregate(2)
        quantise(0)
        nc.vector.tensor_copy(out=b_sorted[:], in_=b_rows[:].rearrange("p (i e) -> p e i", e=8))
        bt = psum.tile([P, 8, P], BF16, name="bt", tag="bank")
        for e in range(8):
            nc.tensor.transpose(bt[:, e, :], b_sorted[:, e, :], ident[:])
        nc.vector.tensor_copy(out=bias[:], in_=bt[:, :, 0:3].rearrange("p e c -> p c e"))
        bt1 = psum.tile([P, 8, P], BF16, name="bt1", tag="bank")
        for s in range(8):
            nc.tensor.transpose(bt1[:, s, :], b_rows[:, P * s:P * (s + 1)], ident[:])
        nc.vector.tensor_copy(out=bias1[:].rearrange("p c s -> p (c s)").unsqueeze(2), in_=bt1[:, :, 3:4])
        aggregate(3)
        quantise(1)

        o2 = out.rearrange("a o w b -> (a o) (w b)")
        ov = o2.rearrange("(c i e) w -> c i (e w)", c=4, i=P, e=8)
        ow = o2.rearrange("(c s p) w -> c p s w", c=8, s=4, p=P)
        s_sb = [keep.tile([P, 8, P], F32, name="s%d" % c) for c in range(3)]
        o_pair = [keep.tile([P, 8, V], F32, name="op%d" % c) for c in range(3)]
        o_sb = [keep.tile([P, 4, V], F32, name="o%d" % c) for c in range(2)]
        accs = {}

        def passes(n):
            g0, ng, n0, nw = PIECES[n]
            for g, col in ((g, col) for g in range(g0, g0 + ng) for col in range(nw // 512)):
                c = n0 // 512 + col
                if g == 0:
                    accs[c] = psum.tile([P, 512], F32, name="acc%d" % c, tag="bank")
                nc.tensor.matmul_mx(
                    out=accs[c][:],
                    lhsT=acodes[:, g, :].bitcast(FP8X4),
                    lhsT_scale=aplane[:, g, :],
                    rhs=w_sb[n][:, g - g0, 2048 * col:2048 * (col + 1)].bitcast(FP8X4),
                    rhs_scale=planes[4 * (g % 4):P, g // 4, 512 * c:512 * (c + 1)],
                    start=(g == 0),
                    stop=(g == G - 1),
                )

        def finish(pairs):
            for c in pairs:
                for h in range(2):
                    nc.scalar.copy(out=s_sb[c][:, :, 64 * h:64 * (h + 1)],
                                   in_=accs[2 * c + h][:].rearrange("p (i e) -> p e i", e=8))
            for c in pairs:
                for h in range(2):
                    z = psum.tile([P, 4, V], F32, name="z", tag="bank")
                    for e in range(4):
                        nc.tensor.transpose(z[:, e, :], s_sb[c][:, 4 * h + e, :], ident32[:])
                    nc.vector.tensor_tensor(out=o_pair[c][:, 4 * h:4 * h + 4, :], in0=z[:],
                                            in1=bias[:, c, 4 * h:4 * h + 4].unsqueeze(2).to_broadcast([P, 4, V]), op=ADD)

        direct = {}

        def passes_direct(n):
            g0, ng, n0, nw = PIECES[n]
            for g, col in ((g, col) for g in range(g0, g0 + ng) for col in range(nw // P)):
                jj = n0 // P + col
                if g == 0 and jj % 2 == 0:
                    direct[jj // 2] = psum.tile([P, 2, V], F32, name="d%d" % (jj // 2), tag="bank")
                nc.tensor.matmul_mx(
                    out=direct[jj // 2][:, jj % 2, :],
                    lhsT=w_sb[n][:, g - g0, 512 * col:512 * (col + 1)].bitcast(FP8X4),
                    lhsT_scale=planes[4 * (g % 4):P, g // 4, P * jj:P * (jj + 1)],
                    rhs=acodes[:, g, :].bitcast(FP8X4),
                    rhs_scale=aplane[:, g, :],
                    start=(g == 0 and jj % 2 == 0),
                    stop=(g == G - 1 and jj % 2 == 1),
                )

        def finish_direct(c):
            lo = direct[2 * c]
            hi = direct[2 * c + 1]
            nc.vector.tensor_tensor(out=o_sb[c - 6][:, 0:2, :], in0=lo[:],
                                    in1=bias1[:, c - 6, 0:2].unsqueeze(2).to_broadcast([P, 2, V]), op=ADD)
            for s in range(2, 4):
                nc.scalar.activation(out=o_sb[c - 6][:, s, :], in_=hi[:, s - 2, :], func=IDENT,
                                     bias=bias1[:, c - 6, s:s + 1], scale=1.0)

        for n in range(4):
            passes(n)
        finish((0, 1))
        for n in range(4, 8):
            passes(n)
        finish((2,))
        for n in range(8, 13):
            passes_direct(n)
        finish_direct(6)
        passes_direct(13)
        finish_direct(7)

        for c in range(3):
            nc.sync.dma_start(out=ov[c], in_=o_pair[c][:].rearrange("p e w -> p (e w)"))
        for c in range(6, 8):
            nc.sync.dma_start(out=ow[c], in_=o_sb[c - 6][:])
